import numpy as np
import ml_dtypes


def mxq(x, axis, fmt="e4m3"):
    dtype, down = {"e4m3": (ml_dtypes.float8_e4m3fn, 7), "e5m2": (ml_dtypes.float8_e5m2, 14)}[fmt]
    v = np.moveaxis(np.asarray(x, np.float32).astype(ml_dtypes.bfloat16).astype(np.float64), axis, -1)
    blocks = v.reshape(v.shape[:-1] + (-1, 32))
    amax = np.abs(blocks).max(-1, keepdims=True)
    byte = np.maximum(np.where(amax > 0, np.frexp(amax)[1] - 1 + 127, 0) - down, 1)
    scale = np.exp2(byte - 127.0)
    codes = (blocks / scale).astype(np.float32).astype(dtype).astype(np.float64)
    return np.moveaxis((codes * scale).reshape(v.shape), -1, axis)


WIDE = False


def mx_kscale(k):
    if not WIDE:
        return np.ones(k)
    levels = np.array([10, -10, 5, -5, 0])
    a = np.random.permutation(np.resize(levels, k // 512 * 4)).reshape(k // 512, 4)
    idx = np.arange(k)
    return np.exp2(a[idx // 512, idx % 128 // 32])


BF16 = ml_dtypes.bfloat16


def bf(x):
    return np.asarray(x, np.float32).astype(BF16)


def f64(x):
    return np.asarray(x).astype(np.float64)


N, C, D, H, W = 2, 16, 512, 16, 16
EPS = 1e-5


def setup_inputs():
    t = np.minimum(mx_kscale(D), 1.0) ** 2
    sig0 = 0.01 * (0.5 + np.random.random_sample((C, D)))
    sig = sig0 * t
    r = np.exp2(np.round(np.log2((sig / np.sqrt(sig**2 + EPS)) / (sig0 / np.sqrt(sig0**2 + EPS)))))
    mu = np.random.standard_normal((C, D))
    z = np.random.standard_normal((N, C, D, H, W))
    x = ((z + mu[None, :, :, None, None]) * sig[None, :, :, None, None]).reshape(N, C * D, H, W)
    weight = (np.eye(D)[None] + np.random.standard_normal((C, D, D)) / np.sqrt(D)) / r[:, None, :]
    return {"x": bf(x), "weight": bf(weight), "bias": bf(np.random.standard_normal(C * D) * 0.3)}


def reference(x, weight, bias):
    x, weight, bias = f64(x), f64(weight), f64(bias)
    n, cd, h, w = x.shape
    c = weight.shape[0]
    d = cd // c
    mean = np.mean(x, axis=(0, 2, 3), keepdims=True)
    var = np.mean(np.square(x - mean), axis=(0, 2, 3), keepdims=True)
    xn = (x - mean) / np.sqrt(var + EPS)
    xg = xn.reshape(n, c, d, h * w)
    out = mxq(weight, 2, "e4m3")[None] @ mxq(xg, 2, "e4m3")
    return out.reshape(n, cd, h, w) + bias[None, :, None, None]

@@ -1,0 +1,270 @@
+from contextlib import ExitStack
+
+import concourse.mybir as mybir
+from concourse.masks import make_identity
+
+F32 = mybir.dt.float32
+BF16 = mybir.dt.bfloat16
+U32 = mybir.dt.uint32
+U8 = mybir.dt.uint8
+FP8X4 = mybir.dt.float8_e4m3fn_x4
+ALU = mybir.AluOpType
+ACT = mybir.ActivationFunctionType
+
+P = 128
+NCAP = 16
+D = 512
+NB = 2
+HW = 256
+COLS = NB * HW
+EPS = 1e-5
+FLOPS = 2 * NCAP * D * D * COLS
+
+BATCHES = [[0], [1]] + [[c, c + 1] for c in range(2, NCAP, 2)]
+UPFRONT = 7
+G_COLS = 320
+V_COLS = 0
+END_V_COLS = 352
+END_FROM = 14
+
+
+def rg_split(j):
+    if j >= END_FROM:
+        return 0, COLS - END_V_COLS, END_V_COLS
+    return G_COLS, COLS - G_COLS - V_COLS, V_COLS
+
+
+def tile_caps_bn_kernel(tc, x, weight, bias, out):
+    nc = tc.nc
+    xv = x.rearrange("n (c p t) h w -> c p n (t h w)", c=NCAP, p=P, t=4)
+    wv = weight.rearrange("c (m a) i -> c m (a i)", m=P, a=4)
+    ov = out.rearrange("n (c m a) h w -> c m n (a h w)", c=NCAP, m=P, a=4)
+    ova = out.rearrange("n (c m a) h w -> c a m n (h w)", c=NCAP, m=P, a=4)
+    bv = bias.rearrange("(c m a) -> m c a", c=NCAP, m=P, a=4)
+
+    with ExitStack() as ctx:
+        const = ctx.enter_context(tc.tile_pool(name="const", bufs=1))
+        xpool = ctx.enter_context(tc.tile_pool(name="xpool", bufs=UPFRONT + 2))
+        wpool = ctx.enter_context(tc.tile_pool(name="wpool", bufs=UPFRONT))
+        work = ctx.enter_context(tc.tile_pool(name="work", bufs=3))
+        small = ctx.enter_context(tc.tile_pool(name="small", bufs=3))
+        opool = ctx.enter_context(tc.tile_pool(name="opool", bufs=3))
+        pst = ctx.enter_context(tc.psum_pool(name="pst", bufs=2))
+        psa = ctx.enter_context(tc.psum_pool(name="psa", bufs=6))
+        ctx.enter_context(tc.manual_schedule())
+
+        warm = const.tile([P, 2], F32)
+        nc.vector.memset(warm[:, 0:1], 1.0)
+        nc.scalar.activation(out=warm[:, 1:2], in_=warm[:, 0:1], func=ACT.Sqrt)
+        ident = const.tile([P, P], F32)
+        make_identity(nc, ident[:])
+        bias_b = const.tile([P, NCAP * 4], BF16)
+        bias_f = const.tile([P, NCAP * 4], F32)
+        mean = const.tile([P, NCAP * 4], F32)
+        rstd = const.tile([P, NCAP * 4], F32)
+        stats = const.tile([P, NCAP * 4, 6], F32)
+        nc.gpsimd.dma_start(out=bias_b[:].rearrange("m (c a) -> m c a", a=4), in_=bv)
+
+        xs = {}
+        ws = {}
+        wt = {}
+        wg = {}
+        wq = {}
+        wsc = {}
+        xn = {}
+        xg = {}
+        xq = {}
+        xsc = {}
+        acc = {}
+        ob = {}
+        sm = {}
+
+        def load(c):
+            xs[c] = xpool.tile([P, NB, 4 * HW], BF16, name="xs")
+            ws[c] = wpool.tile([P, 4 * D], BF16, name="ws")
+            if c == 0:
+                nc.sync.dma_start(out=xs[c][:, :, 0 : 2 * HW], in_=xv[c][:, :, 0 : 2 * HW])
+                nc.sync.dma_start(out=ws[c][:, 0 : 2 * D], in_=wv[c][:, 0 : 2 * D])
+                nc.sync.dma_start(out=xs[c][:, :, 2 * HW : 4 * HW], in_=xv[c][:, :, 2 * HW : 4 * HW])
+                nc.sync.dma_start(out=ws[c][:, 2 * D : 4 * D], in_=wv[c][:, 2 * D : 4 * D])
+            else:
+                nc.sync.dma_start(out=xs[c][:], in_=xv[c])
+                nc.sync.dma_start(out=ws[c][:], in_=wv[c])
+
+        def pe_t(c):
+            wf = ws[c][:].bitcast(F32).rearrange("p (a q u) -> p a u q", a=4, u=2)
+            for h in range(2):
+                wt[c, h] = pst.tile([P, 2, 2, P], F32, name="wt")
+                for a2 in range(2):
+                    for u in range(2):
+                        nc.tensor.transpose(wt[c, h][:, a2, u, :], wf[:, 2 * h + a2, u, :], ident[:])
+
+        def s_wx(c):
+            wg[c] = work.tile([P, 4 * P * 4], BF16, name="wg", align_bytes=64)
+            wgf = wg[c][:].bitcast(F32).rearrange("p (a m u) -> p a m u", a=4, u=2)
+            for h in range(2):
+                nc.scalar.copy(out=wgf[:, 2 * h : 2 * h + 2, :, :], in_=wt[c, h][:].rearrange("p a u m -> p a m u"))
+
+        def v_wq(c):
+            wq[c] = work.tile([P, 4 * P], U32, name="wq", align_bytes=64)
+            wsc[c] = work.tile([P, 4 * P], U8, name="wsc", align_bytes=64)
+            nc.vector.quantize_mx(out=wq[c][:].bitcast(FP8X4), scales=wsc[c][:], in_=wg[c][:])
+
+        def v_st(c):
+            for t in range(4):
+                nc.vector.bn_stats(out=stats[:, 4 * c + t, :], in_=xs[c][:, :, t * HW : (t + 1) * HW])
+
+        def v_sm_a(b):
+            k0 = 4 * b[0]
+            n = 4 * len(b)
+            st = stats[:, k0 : k0 + n, :]
+            d = small.tile([P, 8], F32, name="sm_d")
+            e = small.tile([P, 8], F32, name="sm_e")
+            v = small.tile([P, 8], F32, name="sm_v")
+            nc.vector.tensor_tensor(out=d[:, 0:n], in0=st[:, :, 1], in1=st[:, :, 4], op=ALU.subtract)
+            nc.vector.scalar_tensor_tensor(out=v[:, 0:n], in0=st[:, :, 2], scalar=COLS * EPS, in1=st[:, :, 5], op0=ALU.add, op1=ALU.add)
+            nc.vector.scalar_tensor_tensor(out=e[:, 0:n], in0=d[:, 0:n], scalar=COLS / 4.0, in1=d[:, 0:n], op0=ALU.mult, op1=ALU.mult)
+            nc.vector.scalar_tensor_tensor(out=mean[:, k0 : k0 + n], in0=d[:, 0:n], scalar=0.5, in1=st[:, :, 4], op0=ALU.mult, op1=ALU.add)
+            nc.vector.tensor_tensor(out=v[:, 0:n], in0=v[:, 0:n], in1=e[:, 0:n], op=ALU.add)
+            sm[b[0]] = v
+
+        def s_sm(b):
+            n = 4 * len(b)
+            v = sm[b[0]]
+            nc.scalar.activation(out=v[:, 0:n], in_=v[:, 0:n], func=ACT.Sqrt, scale=1.0 / COLS)
+
+        def v_sm_b(b):
+            k0 = 4 * b[0]
+            n = 4 * len(b)
+            nc.vector.reciprocal(out=rstd[:, k0 : k0 + n], in_=sm[b[0]][:, 0:n])
+
+        def v_nm(c):
+            xn[c] = work.tile([P, 4, COLS], BF16, name="xn")
+            xg[c] = work.tile([P, COLS, 4], BF16, name="xg", align_bytes=64)
+            for t in range(4):
+                k = 4 * c + t
+                nc.vector.tensor_scalar(
+                    out=xn[c][:, t, :].rearrange("p (n w) -> p n w", n=NB),
+                    in0=xs[c][:, :, t * HW : (t + 1) * HW],
+                    scalar1=mean[:, k : k + 1],
+                    scalar2=rstd[:, k : k + 1],
+                    op0=ALU.subtract,
+                    op1=ALU.mult,
+                )
+
+        def rg_views(c, c0, c1):
+            dst = xg[c][:, c0:c1, :].rearrange("p (c i) t -> p c t i", i=4)
+            src = xn[c][:, :, c0:c1].rearrange("p t (c i) -> p c t i", i=4)
+            return dst, src
+
+        def g_rg(c):
+            g, s, v = rg_split(c)
+            if g > 0:
+                nc.gpsimd.tensor_scalar(
+                    out=xg[c][:, 0:g, :],
+                    in0=xn[c][:, :, 0:g].rearrange("p t w -> p w t"),
+                    scalar1=1.0,
+                    scalar2=0.0,
+                    op0=ALU.mult,
+                    op1=ALU.add,
+                )
+
+        def s_rg(c):
+            g, s, v = rg_split(c)
+            if s > 0:
+                dst, src = rg_views(c, g, g + s)
+                nc.scalar.copy(out=dst, in_=src)
+
+        def v_rg(c):
+            g, s, v = rg_split(c)
+            if v > 0:
+                dst, src = rg_views(c, g + s, COLS)
+                nc.vector.tensor_copy(out=dst, in_=src)
+
+        def v_xq(c):
+            xq[c] = work.tile([P, COLS], U32, name="xq", align_bytes=64)
+            xsc[c] = work.tile([P, COLS], U8, name="xsc", align_bytes=64)
+            nc.vector.quantize_mx(out=xq[c][:].bitcast(FP8X4), scales=xsc[c][:], in_=xg[c][:].rearrange("p w t -> p (w t)"))
+
+        def pe_mm(c):
+            for a in range(4):
+                acc[c, a] = psa.tile([P, COLS], F32, name="acc")
+                nc.tensor.matmul_mx(
+                    out=acc[c, a][:],
+                    lhsT=wq[c][:, a * P : (a + 1) * P].bitcast(FP8X4),
+                    lhsT_scale=wsc[c][:, a * P : (a + 1) * P],
+                    rhs=xq[c][:].bitcast(FP8X4),
+                    rhs_scale=xsc[c][:],
+                    start=True,
+                    stop=True,
+                )
+
+        def ox(c, a, on_vector):
+            if c not in ob:
+                ob[c] = opool.tile([P, NB, 4, HW], F32, name="ob")
+            k = 4 * c + a
+            src = acc[c, a][:].rearrange("p (n w) -> p n w", n=NB)
+            if on_vector:
+                nc.vector.tensor_scalar(out=ob[c][:, :, a, :], in0=src, scalar1=bias_f[:, k : k + 1], scalar2=None, op0=ALU.add)
+            else:
+                nc.scalar.activation(out=ob[c][:, :, a, :], in_=src, func=ACT.Identity, bias=bias_f[:, k : k + 1], scale=1.0)
+
+        batch_end = {}
+        for b in BATCHES:
+            batch_end[b[-1]] = b
+
+        for c in range(UPFRONT):
+            load(c)
+        pe_t(0)
+        pending = []
+        for j in range(-2, NCAP + 1):
+            if 0 <= j < NCAP:
+                v_nm(j)
+                g_rg(j)
+            if j + 2 < NCAP:
+                s_wx(j + 2)
+            if j + 3 < NCAP:
+                pe_t(j + 3)
+            b = None
+            if j + 2 < NCAP:
+                v_st(j + 2)
+                b = batch_end.get(j + 2)
+            for pb in pending:
+                v_sm_b(pb)
+            pending = []
+            if 0 <= j < NCAP:
+                s_rg(j)
+            if b is not None:
+                v_sm_a(b)
+            if 0 <= j < NCAP:
+                v_rg(j)
+            if 0 <= j + 1 < NCAP:
+                v_wq(j + 1)
+            if j == 0:
+                nc.scalar.copy(out=bias_f[:], in_=bias_b[:])
+            c = j - 1
+            late = c >= END_FROM
+            if 0 <= c < NCAP - 1:
+                ox(c, 0, False)
+                ox(c, 1, False)
+            if b is not None:
+                s_sm(b)
+            if 0 <= j < NCAP:
+                v_xq(j)
+            if b is not None:
+                if b[0] == j + 1:
+                    v_sm_b(b)
+                else:
+                    pending.append(b)
+            if 0 <= c < NCAP - 1:
+                ox(c, 2, late)
+                ox(c, 3, late)
+                nc.sync.dma_start(out=ov[c], in_=ob[c][:].rearrange("p n a w -> p n (a w)"))
+                if c + UPFRONT < NCAP:
+                    load(c + UPFRONT)
+            if c == NCAP - 1:
+                for a in range(4):
+                    ox(c, a, a % 2 == 1)
+                    nc.sync.dma_start(out=ova[c, a], in_=ob[c][:, :, a, :])
+            if 0 <= j < NCAP:
+                pe_mm(j)

@@ -22,8 +22,8 @@ FLOPS = 2 * NCAP * D * D * COLS
 
 BATCHES = [[0], [1]] + [[c, c + 1] for c in range(2, NCAP, 2)]
 UPFRONT = 7
-G_COLS = 320
-V_COLS = 0
+G_COLS = 0
+V_COLS = 224
 END_V_COLS = 352
 END_FROM = 14
 

@@ -20,7 +20,6 @@ COLS = NB * HW
 EPS = 1e-5
 FLOPS = 2 * NCAP * D * D * COLS
 
-BATCHES = [[0], [1]] + [[c, c + 1] for c in range(2, NCAP, 2)]
 UPFRONT = 7
 G_COLS = 0
 V_COLS = 224
@@ -48,14 +47,14 @@ def tile_caps_bn_kernel(tc, x, weight, bias, out):
         wpool = ctx.enter_context(tc.tile_pool(name="wpool", bufs=UPFRONT))
         work = ctx.enter_context(tc.tile_pool(name="work", bufs=3))
         small = ctx.enter_context(tc.tile_pool(name="small", bufs=3))
-        opool = ctx.enter_context(tc.tile_pool(name="opool", bufs=3))
-        pst = ctx.enter_context(tc.psum_pool(name="pst", bufs=2))
-        psa = ctx.enter_context(tc.psum_pool(name="psa", bufs=6))
+        opool = ctx.enter_context(tc.tile_pool(name="opool", bufs=6))
+        pst = ctx.enter_context(tc.psum_pool(name="pst", bufs=4))
+        psa = ctx.enter_context(tc.psum_pool(name="psa", bufs=4))
+        wqpool = ctx.enter_context(tc.tile_pool(name="wqpool", bufs=4))
         ctx.enter_context(tc.manual_schedule())
 
-        warm = const.tile([P, 2], F32)
-        nc.vector.memset(warm[:, 0:1], 1.0)
-        nc.scalar.activation(out=warm[:, 1:2], in_=warm[:, 0:1], func=ACT.Sqrt)
+        expo = const.tile([P, 4], F32)
+        nc.gpsimd.memset(expo[:], -0.5)
         ident = const.tile([P, P], F32)
         make_identity(nc, ident[:])
         bias_b = const.tile([P, NCAP * 4], BF16)
@@ -63,7 +62,6 @@ def tile_caps_bn_kernel(tc, x, weight, bias, out):
         mean = const.tile([P, NCAP * 4], F32)
         rstd = const.tile([P, NCAP * 4], F32)
         stats = const.tile([P, NCAP * 4, 6], F32)
-        nc.gpsimd.dma_start(out=bias_b[:].rearrange("m (c a) -> m c a", a=4), in_=bv)
 
         xs = {}
         ws = {}
@@ -77,7 +75,6 @@ def tile_caps_bn_kernel(tc, x, weight, bias, out):
         xsc = {}
         acc = {}
         ob = {}
-        sm = {}
 
         def load(c):
             xs[c] = xpool.tile([P, NB, 4 * HW], BF16, name="xs")
@@ -106,37 +103,28 @@ def tile_caps_bn_kernel(tc, x, weight, bias, out):
                 nc.scalar.copy(out=wgf[:, 2 * h : 2 * h + 2, :, :], in_=wt[c, h][:].rearrange("p a u m -> p a m u"))
 
         def v_wq(c):
-            wq[c] = work.tile([P, 4 * P], U32, name="wq", align_bytes=64)
-            wsc[c] = work.tile([P, 4 * P], U8, name="wsc", align_bytes=64)
+            wq[c] = wqpool.tile([P, 4 * P], U32, name="wq", align_bytes=64)
+            wsc[c] = wqpool.tile([P, 4 * P], U8, name="wsc", align_bytes=64)
             nc.vector.quantize_mx(out=wq[c][:].bitcast(FP8X4), scales=wsc[c][:], in_=wg[c][:])
 
         def v_st(c):
             for t in range(4):
                 nc.vector.bn_stats(out=stats[:, 4 * c + t, :], in_=xs[c][:, :, t * HW : (t + 1) * HW])
 
-        def v_sm_a(b):
-            k0 = 4 * b[0]
-            n = 4 * len(b)
-            st = stats[:, k0 : k0 + n, :]
-            d = small.tile([P, 8], F32, name="sm_d")
-            e = small.tile([P, 8], F32, name="sm_e")
-            v = small.tile([P, 8], F32, name="sm_v")
-            nc.vector.tensor_tensor(out=d[:, 0:n], in0=st[:, :, 1], in1=st[:, :, 4], op=ALU.subtract)
-            nc.vector.scalar_tensor_tensor(out=v[:, 0:n], in0=st[:, :, 2], scalar=COLS * EPS, in1=st[:, :, 5], op0=ALU.add, op1=ALU.add)
-            nc.vector.scalar_tensor_tensor(out=e[:, 0:n], in0=d[:, 0:n], scalar=COLS / 4.0, in1=d[:, 0:n], op0=ALU.mult, op1=ALU.mult)
-            nc.vector.scalar_tensor_tensor(out=mean[:, k0 : k0 + n], in0=d[:, 0:n], scalar=0.5, in1=st[:, :, 4], op0=ALU.mult, op1=ALU.add)
-            nc.vector.tensor_tensor(out=v[:, 0:n], in0=v[:, 0:n], in1=e[:, 0:n], op=ALU.add)
-            sm[b[0]] = v
-
-        def s_sm(b):
-            n = 4 * len(b)
-            v = sm[b[0]]
-            nc.scalar.activation(out=v[:, 0:n], in_=v[:, 0:n], func=ACT.Sqrt, scale=1.0 / COLS)
-
-        def v_sm_b(b):
-            k0 = 4 * b[0]
-            n = 4 * len(b)
-            nc.vector.reciprocal(out=rstd[:, k0 : k0 + n], in_=sm[b[0]][:, 0:n])
+        def g_sm(c):
+            k0 = 4 * c
+            st = stats[:, k0 : k0 + 4, :]
+            d = small.tile([P, 4], F32, name="sm_d")
+            s2 = small.tile([P, 4], F32, name="sm_s")
+            dd = small.tile([P, 4], F32, name="sm_q")
+            nc.gpsimd.tensor_tensor(out=d[:], in0=st[:, :, 1], in1=st[:, :, 4], op=ALU.subtract)
+            nc.gpsimd.tensor_tensor(out=s2[:], in0=st[:, :, 2], in1=st[:, :, 5], op=ALU.add)
+            nc.gpsimd.tensor_scalar(out=d[:], in0=d[:], scalar1=0.5, scalar2=0.0, op0=ALU.mult, op1=ALU.add)
+            nc.gpsimd.tensor_scalar(out=s2[:], in0=s2[:], scalar1=1.0 / COLS, scalar2=EPS, op0=ALU.mult, op1=ALU.add)
+            nc.gpsimd.tensor_tensor(out=dd[:], in0=d[:], in1=d[:], op=ALU.mult)
+            nc.gpsimd.tensor_tensor(out=mean[:, k0 : k0 + 4], in0=d[:], in1=st[:, :, 4], op=ALU.add)
+            nc.gpsimd.tensor_tensor(out=dd[:], in0=dd[:], in1=s2[:], op=ALU.add)
+            nc.gpsimd.tensor_tensor(out=rstd[:, k0 : k0 + 4], in0=dd[:], in1=expo[:], op=ALU.pow)
 
         def v_nm(c):
             xn[c] = work.tile([P, 4, COLS], BF16, name="xn")
@@ -209,62 +197,43 @@ def tile_caps_bn_kernel(tc, x, weight, bias, out):
             else:
                 nc.scalar.activation(out=ob[c][:, :, a, :], in_=src, func=ACT.Identity, bias=bias_f[:, k : k + 1], scale=1.0)
 
-        batch_end = {}
-        for b in BATCHES:
-            batch_end[b[-1]] = b
+        def ox_on_vector(c):
+            return 2 if c >= NCAP - 2 else 0
 
         for c in range(UPFRONT):
             load(c)
-        pe_t(0)
-        pending = []
-        for j in range(-2, NCAP + 1):
-            if 0 <= j < NCAP:
-                v_nm(j)
-                g_rg(j)
-            if j + 2 < NCAP:
-                s_wx(j + 2)
-            if j + 3 < NCAP:
-                pe_t(j + 3)
-            b = None
-            if j + 2 < NCAP:
-                v_st(j + 2)
-                b = batch_end.get(j + 2)
-            for pb in pending:
-                v_sm_b(pb)
-            pending = []
-            if 0 <= j < NCAP:
-                s_rg(j)
-            if b is not None:
-                v_sm_a(b)
-            if 0 <= j < NCAP:
-                v_rg(j)
-            if 0 <= j + 1 < NCAP:
-                v_wq(j + 1)
-            if j == 0:
-                nc.scalar.copy(out=bias_f[:], in_=bias_b[:])
-            c = j - 1
-            late = c >= END_FROM
-            if 0 <= c < NCAP - 1:
-                ox(c, 0, False)
-                ox(c, 1, False)
-            if b is not None:
-                s_sm(b)
-            if 0 <= j < NCAP:
-                v_xq(j)
-            if b is not None:
-                if b[0] == j + 1:
-                    v_sm_b(b)
-                else:
-                    pending.append(b)
-            if 0 <= c < NCAP - 1:
-                ox(c, 2, late)
-                ox(c, 3, late)
-                nc.sync.dma_start(out=ov[c], in_=ob[c][:].rearrange("p n a w -> p n (a w)"))
-                if c + UPFRONT < NCAP:
-                    load(c + UPFRONT)
-            if c == NCAP - 1:
+            if c == 2:
+                nc.sync.dma_start(out=bias_b[:].rearrange("m (c a) -> m c a", a=4), in_=bv)
+        for i in range(-4, NCAP + 1):
+            if 0 <= i < NCAP:
+                v_xq(i)
+            c = i - 1
+            if 0 <= c < NCAP:
+                on_v = [1, 3][: ox_on_vector(c)]
+                last = c == NCAP - 1
                 for a in range(4):
-                    ox(c, a, a % 2 == 1)
-                    nc.sync.dma_start(out=ova[c, a], in_=ob[c][:, :, a, :])
-            if 0 <= j < NCAP:
-                pe_mm(j)
+                    ox(c, a, a in on_v)
+                    if last:
+                        nc.sync.dma_start(out=ova[c, a], in_=ob[c][:, :, a, :])
+                if not last:
+                    nc.sync.dma_start(out=ov[c], in_=ob[c][:].rearrange("p n a w -> p n (a w)"))
+                    if c + UPFRONT < NCAP:
+                        load(c + UPFRONT)
+            if 0 <= i < NCAP:
+                pe_mm(i)
+            if 0 <= i + 4 < NCAP:
+                pe_t(i + 4)
+            if 0 <= i + 1 < NCAP:
+                v_nm(i + 1)
+            if 0 <= i + 3 < NCAP:
+                v_st(i + 3)
+                g_sm(i + 3)
+            if 0 <= i + 1 < NCAP:
+                s_rg(i + 1)
+                v_rg(i + 1)
+            if 0 <= i + 3 < NCAP:
+                s_wx(i + 3)
+            if i == 0:
+                nc.scalar.copy(out=bias_f[:], in_=bias_b[:])
+            if 0 <= i + 2 < NCAP:
+                v_wq(i + 2)

@@ -20,17 +20,11 @@ COLS = NB * HW
 EPS = 1e-5
 FLOPS = 2 * NCAP * D * D * COLS
 
-UPFRONT = 7
-G_COLS = 0
-V_COLS = 224
-END_V_COLS = 352
-END_FROM = 14
-
-
-def rg_split(j):
-    if j >= END_FROM:
-        return 0, COLS - END_V_COLS, END_V_COLS
-    return G_COLS, COLS - G_COLS - V_COLS, V_COLS
+BATCHES = [[0], [1]] + [[c, c + 1] for c in range(2, NCAP, 2)]
+UPFRONT = 8
+ST_LEAD = 4
+V_COLS = [160,192,224,224,224,224,224,224,224,224,224,256,256,512,448,448]
+OX_ON_V = [0,0,0,0,0,0,0,0,0,0,0,0,0,1,1,2]
 
 
 def tile_caps_bn_kernel(tc, x, weight, bias, out):
@@ -53,8 +47,9 @@ def tile_caps_bn_kernel(tc, x, weight, bias, out):
         wqpool = ctx.enter_context(tc.tile_pool(name="wqpool", bufs=4))
         ctx.enter_context(tc.manual_schedule())
 
-        expo = const.tile([P, 4], F32)
-        nc.gpsimd.memset(expo[:], -0.5)
+        warm = const.tile([P, 2], F32)
+        nc.vector.memset(warm[:, 0:1], 1.0)
+        nc.scalar.activation(out=warm[:, 1:2], in_=warm[:, 0:1], func=ACT.Sqrt)
         ident = const.tile([P, P], F32)
         make_identity(nc, ident[:])
         bias_b = const.tile([P, NCAP * 4], BF16)
@@ -75,6 +70,7 @@ def tile_caps_bn_kernel(tc, x, weight, bias, out):
         xsc = {}
         acc = {}
         ob = {}
+        sm = {}
 
         def load(c):
             xs[c] = xpool.tile([P, NB, 4 * HW], BF16, name="xs")
@@ -107,24 +103,46 @@ def tile_caps_bn_kernel(tc, x, weight, bias, out):
             wsc[c] = wqpool.tile([P, 4 * P], U8, name="wsc", align_bytes=64)
             nc.vector.quantize_mx(out=wq[c][:].bitcast(FP8X4), scales=wsc[c][:], in_=wg[c][:])
 
-        def v_st(c):
-            for t in range(4):
-                nc.vector.bn_stats(out=stats[:, 4 * c + t, :], in_=xs[c][:, :, t * HW : (t + 1) * HW])
+        def v_sm_piece(b, k):
+            k0 = 4 * b[0]
+            n = 4 * len(b)
+            st = stats[:, k0 : k0 + n, :]
+            if k == 0:
+                sm[b[0], "d"] = small.tile([P, 8], F32, name="sm_d")
+                sm[b[0], "e"] = small.tile([P, 8], F32, name="sm_e")
+                sm[b[0]] = small.tile([P, 8], F32, name="sm_v")
+            d = sm[b[0], "d"][:, 0:n]
+            e = sm[b[0], "e"][:, 0:n]
+            v = sm[b[0]][:, 0:n]
+            if k == 0:
+                nc.vector.tensor_tensor(out=d, in0=st[:, :, 1], in1=st[:, :, 4], op=ALU.subtract)
+            elif k == 1:
+                nc.vector.scalar_tensor_tensor(out=v, in0=st[:, :, 2], scalar=COLS * EPS, in1=st[:, :, 5], op0=ALU.add, op1=ALU.add)
+            elif k == 2:
+                nc.vector.scalar_tensor_tensor(out=e, in0=d, scalar=COLS / 4.0, in1=d, op0=ALU.mult, op1=ALU.mult)
+            elif k == 3:
+                nc.vector.scalar_tensor_tensor(out=mean[:, k0 : k0 + n], in0=d, scalar=0.5, in1=st[:, :, 4], op0=ALU.mult, op1=ALU.add)
+            else:
+                nc.vector.tensor_tensor(out=v, in0=v, in1=e, op=ALU.add)
 
-        def g_sm(c):
-            k0 = 4 * c
-            st = stats[:, k0 : k0 + 4, :]
-            d = small.tile([P, 4], F32, name="sm_d")
-            s2 = small.tile([P, 4], F32, name="sm_s")
-            dd = small.tile([P, 4], F32, name="sm_q")
-            nc.gpsimd.tensor_tensor(out=d[:], in0=st[:, :, 1], in1=st[:, :, 4], op=ALU.subtract)
-            nc.gpsimd.tensor_tensor(out=s2[:], in0=st[:, :, 2], in1=st[:, :, 5], op=ALU.add)
-            nc.gpsimd.tensor_scalar(out=d[:], in0=d[:], scalar1=0.5, scalar2=0.0, op0=ALU.mult, op1=ALU.add)
-            nc.gpsimd.tensor_scalar(out=s2[:], in0=s2[:], scalar1=1.0 / COLS, scalar2=EPS, op0=ALU.mult, op1=ALU.add)
-            nc.gpsimd.tensor_tensor(out=dd[:], in0=d[:], in1=d[:], op=ALU.mult)
-            nc.gpsimd.tensor_tensor(out=mean[:, k0 : k0 + 4], in0=d[:], in1=st[:, :, 4], op=ALU.add)
-            nc.gpsimd.tensor_tensor(out=dd[:], in0=dd[:], in1=s2[:], op=ALU.add)
-            nc.gpsimd.tensor_tensor(out=rstd[:, k0 : k0 + 4], in0=dd[:], in1=expo[:], op=ALU.pow)
+        def v_st_sm(c, b):
+            pieces = [[0, 1], [2, 3], [4], []]
+            for t in range(4):
+                if c is not None:
+                    nc.vector.bn_stats(out=stats[:, 4 * c + t, :], in_=xs[c][:, :, t * HW : (t + 1) * HW])
+                if b is not None:
+                    for k in pieces[t]:
+                        v_sm_piece(b, k)
+
+        def s_sm(b):
+            n = 4 * len(b)
+            v = sm[b[0]]
+            nc.scalar.activation(out=v[:, 0:n], in_=v[:, 0:n], func=ACT.Sqrt, scale=1.0 / COLS)
+
+        def v_sm_b(b):
+            k0 = 4 * b[0]
+            n = 4 * len(b)
+            nc.vector.reciprocal(out=rstd[:, k0 : k0 + n], in_=sm[b[0]][:, 0:n])
 
         def v_nm(c):
             xn[c] = work.tile([P, 4, COLS], BF16, name="xn")
@@ -145,28 +163,14 @@ def tile_caps_bn_kernel(tc, x, weight, bias, out):
             src = xn[c][:, :, c0:c1].rearrange("p t (c i) -> p c t i", i=4)
             return dst, src
 
-        def g_rg(c):
-            g, s, v = rg_split(c)
-            if g > 0:
-                nc.gpsimd.tensor_scalar(
-                    out=xg[c][:, 0:g, :],
-                    in0=xn[c][:, :, 0:g].rearrange("p t w -> p w t"),
-                    scalar1=1.0,
-                    scalar2=0.0,
-                    op0=ALU.mult,
-                    op1=ALU.add,
-                )
-
         def s_rg(c):
-            g, s, v = rg_split(c)
-            if s > 0:
-                dst, src = rg_views(c, g, g + s)
+            if V_COLS[c] < COLS:
+                dst, src = rg_views(c, V_COLS[c], COLS)
                 nc.scalar.copy(out=dst, in_=src)
 
         def v_rg(c):
-            g, s, v = rg_split(c)
-            if v > 0:
-                dst, src = rg_views(c, g + s, COLS)
+            if V_COLS[c] > 0:
+                dst, src = rg_views(c, 0, V_COLS[c])
                 nc.vector.tensor_copy(out=dst, in_=src)
 
         def v_xq(c):
@@ -197,19 +201,25 @@ def tile_caps_bn_kernel(tc, x, weight, bias, out):
             else:
                 nc.scalar.activation(out=ob[c][:, :, a, :], in_=src, func=ACT.Identity, bias=bias_f[:, k : k + 1], scale=1.0)
 
-        def ox_on_vector(c):
-            return 2 if c >= NCAP - 2 else 0
+        batch_end = {}
+        for b in BATCHES:
+            batch_end[b[-1]] = b
 
         for c in range(UPFRONT):
             load(c)
             if c == 2:
                 nc.sync.dma_start(out=bias_b[:].rearrange("m (c a) -> m c a", a=4), in_=bv)
-        for i in range(-4, NCAP + 1):
+        sm_a_next = None
+        sm_b_next = None
+        for i in range(-ST_LEAD, NCAP + 1):
             if 0 <= i < NCAP:
                 v_xq(i)
+            if sm_b_next is not None:
+                v_sm_b(sm_b_next)
+                sm_b_next = None
             c = i - 1
             if 0 <= c < NCAP:
-                on_v = [1, 3][: ox_on_vector(c)]
+                on_v = [1, 3, 2, 0][: OX_ON_V[c]]
                 last = c == NCAP - 1
                 for a in range(4):
                     ox(c, a, a in on_v)
@@ -223,11 +233,16 @@ def tile_caps_bn_kernel(tc, x, weight, bias, out):
                 pe_mm(i)
             if 0 <= i + 4 < NCAP:
                 pe_t(i + 4)
+            if 0 <= i + 2 < NCAP:
+                v_wq(i + 2)
             if 0 <= i + 1 < NCAP:
                 v_nm(i + 1)
-            if 0 <= i + 3 < NCAP:
-                v_st(i + 3)
-                g_sm(i + 3)
+            cs = i + ST_LEAD if i + ST_LEAD < NCAP else None
+            b = sm_a_next
+            sm_a_next = None
+            v_st_sm(cs, b)
+            if cs is not None:
+                sm_a_next = batch_end.get(cs)
             if 0 <= i + 1 < NCAP:
                 s_rg(i + 1)
                 v_rg(i + 1)
@@ -235,5 +250,6 @@ def tile_caps_bn_kernel(tc, x, weight, bias, out):
                 s_wx(i + 3)
             if i == 0:
                 nc.scalar.copy(out=bias_f[:], in_=bias_b[:])
-            if 0 <= i + 2 < NCAP:
-                v_wq(i + 2)
+            if b is not None:
+                s_sm(b)
+                sm_b_next = b

@@ -23,7 +23,8 @@ FLOPS = 2 * NCAP * D * D * COLS
 BATCHES = [[0], [1]] + [[c, c + 1] for c in range(2, NCAP, 2)]
 UPFRONT = 8
 ST_LEAD = 4
-V_COLS = [160,192,224,224,224,224,224,224,224,224,224,256,256,512,448,448]
+V_COLS = [0,0,0,0,0,0,0,0,0,0,0,0,0,512,448,448]
+G_COLS = [320,320,320,320,320,320,320,320,320,320,320,320,320,0,0,0]
 OX_ON_V = [0,0,0,0,0,0,0,0,0,0,0,0,0,1,1,2]
 
 
@@ -125,11 +126,10 @@ def tile_caps_bn_kernel(tc, x, weight, bias, out):
             else:
                 nc.vector.tensor_tensor(out=v, in0=v, in1=e, op=ALU.add)
 
-        def v_st_sm(c, b):
+        def v_st(c, b):
             pieces = [[0, 1], [2, 3], [4], []]
             for t in range(4):
-                if c is not None:
-                    nc.vector.bn_stats(out=stats[:, 4 * c + t, :], in_=xs[c][:, :, t * HW : (t + 1) * HW])
+                nc.vector.bn_stats(out=stats[:, 4 * c + t, :], in_=xs[c][:, :, t * HW : (t + 1) * HW])
                 if b is not None:
                     for k in pieces[t]:
                         v_sm_piece(b, k)
@@ -144,10 +144,12 @@ def tile_caps_bn_kernel(tc, x, weight, bias, out):
             n = 4 * len(b)
             nc.vector.reciprocal(out=rstd[:, k0 : k0 + n], in_=sm[b[0]][:, 0:n])
 
-        def v_nm(c):
+        def v_nm(c, b):
             xn[c] = work.tile([P, 4, COLS], BF16, name="xn")
             xg[c] = work.tile([P, COLS, 4], BF16, name="xg", align_bytes=64)
             for t in range(4):
+                if t == 1 and b is not None:
+                    v_sm_piece(b, 4)
                 k = 4 * c + t
                 nc.vector.tensor_scalar(
                     out=xn[c][:, t, :].rearrange("p (n w) -> p n w", n=NB),
@@ -164,9 +166,22 @@ def tile_caps_bn_kernel(tc, x, weight, bias, out):
             return dst, src
 
         def s_rg(c):
-            if V_COLS[c] < COLS:
-                dst, src = rg_views(c, V_COLS[c], COLS)
+            if V_COLS[c] + G_COLS[c] < COLS:
+                dst, src = rg_views(c, V_COLS[c] + G_COLS[c], COLS)
                 nc.scalar.copy(out=dst, in_=src)
+
+        def g_rg(c):
+            if G_COLS[c] > 0:
+                c0 = V_COLS[c]
+                c1 = c0 + G_COLS[c]
+                nc.gpsimd.tensor_scalar(
+                    out=xg[c][:, c0:c1, :],
+                    in0=xn[c][:, :, c0:c1].rearrange("p t c -> p c t"),
+                    scalar1=1.0,
+                    scalar2=0.0,
+                    op0=ALU.mult,
+                    op1=ALU.add,
+                )
 
         def v_rg(c):
             if V_COLS[c] > 0:
@@ -233,23 +248,36 @@ def tile_caps_bn_kernel(tc, x, weight, bias, out):
                 pe_mm(i)
             if 0 <= i + 4 < NCAP:
                 pe_t(i + 4)
-            if 0 <= i + 2 < NCAP:
-                v_wq(i + 2)
-            if 0 <= i + 1 < NCAP:
-                v_nm(i + 1)
-            cs = i + ST_LEAD if i + ST_LEAD < NCAP else None
             b = sm_a_next
             sm_a_next = None
-            v_st_sm(cs, b)
-            if cs is not None:
-                sm_a_next = batch_end.get(cs)
+            cs = i + ST_LEAD
+            if i + 1 < 0:
+                if 0 <= i + 2:
+                    v_wq(i + 2)
+                v_st(cs, b)
+            else:
+                if b is not None:
+                    v_sm_piece(b, 0)
+                    v_sm_piece(b, 1)
+                if i + 2 < NCAP:
+                    v_wq(i + 2)
+                if b is not None:
+                    v_sm_piece(b, 2)
+                    v_sm_piece(b, 3)
+                if i + 1 < NCAP:
+                    v_nm(i + 1, b)
+            if b is not None:
+                s_sm(b)
+                sm_b_next = b
             if 0 <= i + 1 < NCAP:
+                g_rg(i + 1)
                 s_rg(i + 1)
                 v_rg(i + 1)
+            if 0 <= i + 1 and cs < NCAP:
+                v_st(cs, None)
+            if cs < NCAP:
+                sm_a_next = batch_end.get(cs)
             if 0 <= i + 3 < NCAP:
                 s_wx(i + 3)
             if i == 0:
                 nc.scalar.copy(out=bias_f[:], in_=bias_b[:])
-            if b is not None:
-                s_sm(b)
-                sm_b_next = b

@@ -58,6 +58,8 @@ def tile_caps_bn_kernel(tc, x, weight, bias, out):
         mean = const.tile([P, NCAP * 4], F32)
         rstd = const.tile([P, NCAP * 4], F32)
         stats = const.tile([P, NCAP * 4, 6], F32)
+        sacc = const.tile([P, 4, 2], F32)
+        junk = const.tile([P, NB, HW], BF16)
 
         xs = {}
         ws = {}
@@ -73,17 +75,34 @@ def tile_caps_bn_kernel(tc, x, weight, bias, out):
         ob = {}
         sm = {}
 
-        def load(c):
+        def load_x(c):
             xs[c] = xpool.tile([P, NB, 4 * HW], BF16, name="xs")
+            nc.sync.dma_start(out=xs[c][:], in_=xv[c])
+
+        def load_x_half(c, h):
+            if h == 0:
+                xs[c] = xpool.tile([P, NB, 4 * HW], BF16, name="xs")
+            nc.sync.dma_start(out=xs[c][:, :, 2 * h * HW : 2 * (h + 1) * HW], in_=xv[c][:, :, 2 * h * HW : 2 * (h + 1) * HW])
+
+        def load_w(c):
             ws[c] = wpool.tile([P, 4 * D], BF16, name="ws")
-            if c == 0:
-                nc.sync.dma_start(out=xs[c][:, :, 0 : 2 * HW], in_=xv[c][:, :, 0 : 2 * HW])
-                nc.sync.dma_start(out=ws[c][:, 0 : 2 * D], in_=wv[c][:, 0 : 2 * D])
-                nc.sync.dma_start(out=xs[c][:, :, 2 * HW : 4 * HW], in_=xv[c][:, :, 2 * HW : 4 * HW])
-                nc.sync.dma_start(out=ws[c][:, 2 * D : 4 * D], in_=wv[c][:, 2 * D : 4 * D])
-            else:
-                nc.sync.dma_start(out=xs[c][:], in_=xv[c])
-                nc.sync.dma_start(out=ws[c][:], in_=wv[c])
+            nc.sync.dma_start(out=ws[c][:], in_=wv[c])
+
+        def s_st(c, t):
+            src = xs[c][:, :, t * HW : (t + 1) * HW]
+            shift = xs[c][:, 0, t * HW : t * HW + 1]
+            nc.scalar.activation(out=junk[:], in_=src, func=ACT.Identity, bias=shift, scale=-1.0, accum_out=sacc[:, t, 0:1])
+            nc.scalar.activation(out=junk[:], in_=src, func=ACT.Square, bias=shift, scale=-1.0, accum_out=sacc[:, t, 1:2])
+
+        def v_sm_s(c):
+            sm[c, "e"] = small.tile([P, 8], F32, name="sm_e")
+            sm[c] = small.tile([P, 8], F32, name="sm_v")
+            e = sm[c, "e"][:, 0:4]
+            v = sm[c][:, 0:4]
+            shifts = xs[c][:, 0, :].rearrange("p (t w) -> p t w", t=4)[:, :, 0]
+            nc.vector.scalar_tensor_tensor(out=e, in0=sacc[:, :, 0], scalar=-1.0 / COLS, in1=sacc[:, :, 0], op0=ALU.mult, op1=ALU.mult)
+            nc.vector.scalar_tensor_tensor(out=mean[:, 4 * c : 4 * c + 4], in0=sacc[:, :, 0], scalar=-1.0 / COLS, in1=shifts, op0=ALU.mult, op1=ALU.add)
+            nc.vector.scalar_tensor_tensor(out=v, in0=sacc[:, :, 1], scalar=COLS * EPS, in1=e, op0=ALU.add, op1=ALU.add)
 
         def pe_t(c):
             wf = ws[c][:].bitcast(F32).rearrange("p (a q u) -> p a u q", a=4, u=2)
@@ -220,13 +239,51 @@ def tile_caps_bn_kernel(tc, x, weight, bias, out):
         for b in BATCHES:
             batch_end[b[-1]] = b
 
-        for c in range(UPFRONT):
-            load(c)
-            if c == 2:
-                nc.sync.dma_start(out=bias_b[:].rearrange("m (c a) -> m c a", a=4), in_=bv)
-        sm_a_next = None
+        load_x_half(0, 0)
+        load_x_half(1, 0)
+        load_x_half(0, 1)
+        load_x_half(2, 0)
+        load_x_half(1, 1)
+        load_x_half(2, 1)
+        load_w(0)
+        load_x(3)
+        load_w(1)
+        load_w(2)
+        load_x(4)
+        load_w(3)
+        nc.sync.dma_start(out=bias_b[:].rearrange("m (c a) -> m c a", a=4), in_=bv)
+        for c in range(5, UPFRONT):
+            load_x(c)
+            load_w(c - 1)
+        load_w(UPFRONT - 1)
+
+        pe_t(0)
+        pe_t(1)
+        v_st(0, None)
+        s_st(1, 0)
+        s_st(1, 1)
+        s_st(1, 2)
+        v_st(2, [0])
+        s_sm([0])
+        s_st(1, 3)
+        s_wx(0)
+        v_sm_b([0])
+        v_nm(0, None)
+        g_rg(0)
+        s_rg(0)
+        v_st(3, None)
+        pe_t(2)
+        s_wx(1)
+        pe_t(3)
+        v_sm_s(1)
+        v_wq(0)
+        s_sm([1])
+        v_sm_b([1])
+        v_wq(1)
+        s_wx(2)
+        sm_a_next = [2, 3]
         sm_b_next = None
-        for i in range(-ST_LEAD, NCAP + 1):
+        for i in range(0, NCAP + 1):
             if 0 <= i < NCAP:
                 v_xq(i)
             if sm_b_next is not None:
@@ -243,7 +300,8 @@ def tile_caps_bn_kernel(tc, x, weight, bias, out):
                 if not last:
                     nc.sync.dma_start(out=ov[c], in_=ob[c][:].rearrange("p n a w -> p n (a w)"))
                     if c + UPFRONT < NCAP:
-                        load(c + UPFRONT)
+                        load_x(c + UPFRONT)
+                        load_w(c + UPFRONT)
             if 0 <= i < NCAP:
                 pe_mm(i)
             if 0 <= i + 4 < NCAP:
@@ -251,21 +309,16 @@ def tile_caps_bn_kernel(tc, x, weight, bias, out):
             b = sm_a_next
             sm_a_next = None
             cs = i + ST_LEAD
-            if i + 1 < 0:
-                if 0 <= i + 2:
-                    v_wq(i + 2)
-                v_st(cs, b)
-            else:
-                if b is not None:
-                    v_sm_piece(b, 0)
-                    v_sm_piece(b, 1)
-                if i + 2 < NCAP:
-                    v_wq(i + 2)
-                if b is not None:
-                    v_sm_piece(b, 2)
-                    v_sm_piece(b, 3)
-                if i + 1 < NCAP:
-                    v_nm(i + 1, b)
+            if b is not None:
+                v_sm_piece(b, 0)
+                v_sm_piece(b, 1)
+            if i + 2 < NCAP:
+                v_wq(i + 2)
+            if b is not None:
+                v_sm_piece(b, 2)
+                v_sm_piece(b, 3)
+            if i + 1 < NCAP:
+                v_nm(i + 1, b)
             if b is not None:
                 s_sm(b)
                 sm_b_next = b

@@ -123,6 +123,16 @@ def tile_caps_bn_kernel(tc, x, weight, bias, out):
             wsc[c] = wqpool.tile([P, 4 * P], U8, name="wsc", align_bytes=64)
             nc.vector.quantize_mx(out=wq[c][:].bitcast(FP8X4), scales=wsc[c][:], in_=wg[c][:])
 
+        def v_wq_half(c, h):
+            if h == 0:
+                wq[c] = wqpool.tile([P, 4 * P], U32, name="wq", align_bytes=64)
+                wsc[c] = wqpool.tile([P, 4 * P], U8, name="wsc", align_bytes=64)
+            nc.vector.quantize_mx(
+                out=wq[c][:, 2 * h * P : 2 * (h + 1) * P].bitcast(FP8X4),
+                scales=wsc[c][:, 2 * h * P : 2 * (h + 1) * P],
+                in_=wg[c][:, 8 * h * P : 8 * (h + 1) * P],
+            )
+
         def v_sm_piece(b, k):
             k0 = 4 * b[0]
             n = 4 * len(b)
@@ -313,12 +323,14 @@ def tile_caps_bn_kernel(tc, x, weight, bias, out):
                 v_sm_piece(b, 0)
                 v_sm_piece(b, 1)
             if i + 2 < NCAP:
-                v_wq(i + 2)
+                v_wq_half(i + 2, 0)
             if b is not None:
                 v_sm_piece(b, 2)
                 v_sm_piece(b, 3)
             if i + 1 < NCAP:
                 v_nm(i + 1, b)
+            if i + 2 < NCAP:
+                v_wq_half(i + 2, 1)
             if b is not None:
                 s_sm(b)
                 sm_b_next = b

@@ -217,10 +217,17 @@ def tile_caps_bn_kernel(tc, x, weight, bias, out):
                 dst, src = rg_views(c, 0, V_COLS[c])
                 nc.vector.tensor_copy(out=dst, in_=src)
 
-        def v_xq(c):
-            xq[c] = work.tile([P, COLS], U32, name="xq", align_bytes=64)
-            xsc[c] = work.tile([P, COLS], U8, name="xsc", align_bytes=64)
-            nc.vector.quantize_mx(out=xq[c][:].bitcast(FP8X4), scales=xsc[c][:], in_=xg[c][:].rearrange("p w t -> p (w t)"))
+        def v_xq(c, h):
+            if h == 0:
+                xq[c] = work.tile([P, COLS], U32, name="xq", align_bytes=64)
+                xsc[c] = work.tile([P, COLS], U8, name="xsc", align_bytes=64)
+            c0 = h * COLS // 2
+            c1 = (h + 1) * COLS // 2
+            nc.vector.quantize_mx(
+                out=xq[c][:, c0:c1].bitcast(FP8X4),
+                scales=xsc[c][:, c0:c1],
+                in_=xg[c][:, c0:c1, :].rearrange("p w t -> p (w t)"),
+            )
 
         def pe_mm(c):
             for a in range(4):
@@ -295,7 +302,7 @@ def tile_caps_bn_kernel(tc, x, weight, bias, out):
         sm_b_next = None
         for i in range(0, NCAP + 1):
             if 0 <= i < NCAP:
-                v_xq(i)
+                v_xq(i, 0)
             if sm_b_next is not None:
                 v_sm_b(sm_b_next)
                 sm_b_next = None
@@ -312,25 +319,24 @@ def tile_caps_bn_kernel(tc, x, weight, bias, out):
                     if c + UPFRONT < NCAP:
                         load_x(c + UPFRONT)
                         load_w(c + UPFRONT)
-            if 0 <= i < NCAP:
-                pe_mm(i)
-            if 0 <= i + 4 < NCAP:
-                pe_t(i + 4)
             b = sm_a_next
             sm_a_next = None
             cs = i + ST_LEAD
             if b is not None:
                 v_sm_piece(b, 0)
                 v_sm_piece(b, 1)
-            if i + 2 < NCAP:
-                v_wq_half(i + 2, 0)
+            if 0 <= i < NCAP:
+                v_xq(i, 1)
+                pe_mm(i)
+            if 0 <= i + 4 < NCAP:
+                pe_t(i + 4)
             if b is not None:
                 v_sm_piece(b, 2)
                 v_sm_piece(b, 3)
             if i + 1 < NCAP:
                 v_nm(i + 1, b)
             if i + 2 < NCAP:
-                v_wq_half(i + 2, 1)
+                v_wq(i + 2)
             if b is not None:
                 s_sm(b)
                 sm_b_next = b

@@ -24,7 +24,7 @@ BATCHES = [[0], [1]] + [[c, c + 1] for c in range(2, NCAP, 2)]
 UPFRONT = 8
 ST_LEAD = 4
 V_COLS = [0,0,0,0,0,0,0,0,0,0,0,0,0,512,448,448]
-G_COLS = [320,320,320,320,320,320,320,320,320,320,320,320,320,0,0,0]
+G_COLS = [352,352,352,352,352,352,352,352,352,352,352,352,352,0,0,0]
 OX_ON_V = [0,0,0,0,0,0,0,0,0,0,0,0,0,1,1,2]
 
 

@@ -34,7 +34,7 @@ def tile_caps_bn_kernel(tc, x, weight, bias, out):
     wv = weight.rearrange("c (m a) i -> c m (a i)", m=P, a=4)
     ov = out.rearrange("n (c m a) h w -> c m n (a h w)", c=NCAP, m=P, a=4)
     ova = out.rearrange("n (c m a) h w -> c a m n (h w)", c=NCAP, m=P, a=4)
-    bv = bias.rearrange("(c m a) -> m c a", c=NCAP, m=P, a=4)
+    bv = bias.rearrange("(c o) -> c o", c=NCAP)
 
     with ExitStack() as ctx:
         const = ctx.enter_context(tc.tile_pool(name="const", bufs=1))
@@ -53,7 +53,9 @@ def tile_caps_bn_kernel(tc, x, weight, bias, out):
         nc.scalar.activation(out=warm[:, 1:2], in_=warm[:, 0:1], func=ACT.Sqrt)
         ident = const.tile([P, P], F32)
         make_identity(nc, ident[:])
-        bias_b = const.tile([P, NCAP * 4], BF16)
+        bias_rows = const.tile([P, D], BF16)
+        nc.vector.memset(bias_rows[:], 0.0)
+        bias_am = const.tile([P, 4, P], F32)
         bias_f = const.tile([P, NCAP * 4], F32)
         mean = const.tile([P, NCAP * 4], F32)
         rstd = const.tile([P, NCAP * 4], F32)
@@ -257,6 +259,7 @@ def tile_caps_bn_kernel(tc, x, weight, bias, out):
             batch_end[b[-1]] = b
 
         load_x_half(0, 0)
+        nc.sync.dma_start(out=bias_rows[0:NCAP, :], in_=bv)
         load_x_half(1, 0)
         load_x_half(0, 1)
         load_x_half(2, 0)
@@ -268,12 +271,15 @@ def tile_caps_bn_kernel(tc, x, weight, bias, out):
         load_w(2)
         load_x(4)
         load_w(3)
-        nc.sync.dma_start(out=bias_b[:].rearrange("m (c a) -> m c a", a=4), in_=bv)
         for c in range(5, UPFRONT):
             load_x(c)
             load_w(c - 1)
         load_w(UPFRONT - 1)
 
+        nc.scalar.copy(out=bias_am[:], in_=bias_rows[:].rearrange("q (m a) -> q a m", a=4))
+        bias_t = psa.tile([P, 4, P], F32, name="acc")
+        for a in range(4):
+            nc.tensor.transpose(bias_t[:, a, :], bias_am[:, a, :], ident[:])
         pe_t(0)
         pe_t(1)
         v_st(0, None)
@@ -298,6 +304,7 @@ def tile_caps_bn_kernel(tc, x, weight, bias, out):
         v_sm_b([1])
         v_wq(1)
         s_wx(2)
+        nc.scalar.copy(out=bias_f[:].rearrange("m (c a) -> m c a", a=4), in_=bias_t[:, :, 0:NCAP].rearrange("m a c -> m c a"))
         sm_a_next = [2, 3]
         sm_b_next = None
         for i in range(0, NCAP + 1):
@@ -350,5 +357,3 @@ def tile_caps_bn_kernel(tc, x, weight, bias, out):
                 sm_a_next = batch_end.get(cs)
             if 0 <= i + 3 < NCAP:
                 s_wx(i + 3)
-            if i == 0:
-                nc.scalar.copy(out=bias_f[:], in_=bias_b[:])

@@ -33,7 +33,6 @@ def tile_caps_bn_kernel(tc, x, weight, bias, out):
     xv = x.rearrange("n (c p t) h w -> c p n (t h w)", c=NCAP, p=P, t=4)
     wv = weight.rearrange("c (m a) i -> c m (a i)", m=P, a=4)
     ov = out.rearrange("n (c m a) h w -> c m n (a h w)", c=NCAP, m=P, a=4)
-    ova = out.rearrange("n (c m a) h w -> c a m n (h w)", c=NCAP, m=P, a=4)
     bv = bias.rearrange("(c o) -> c o", c=NCAP)
 
     with ExitStack() as ctx:
@@ -254,6 +253,39 @@ def tile_caps_bn_kernel(tc, x, weight, bias, out):
             else:
                 nc.scalar.activation(out=ob[c][:, :, a, :], in_=src, func=ACT.Identity, bias=bias_f[:, k : k + 1], scale=1.0)
 
+        def v_out(c):
+            for a in range(4):
+                ox(c, a, a in [1, 3, 2, 0][: OX_ON_V[c]])
+            nc.sync.dma_start(out=ov[c], in_=ob[c][:].rearrange("p n a w -> p n (a w)"))
+            if c + UPFRONT < NCAP:
+                load_x(c + UPFRONT)
+                load_w(c + UPFRONT)
+
+        def pe_mm_half(c, n):
+            for g in range(2):
+                acc[c, n, g] = psa.tile([P, 2, HW], F32, name="acc")
+                for a2 in range(2):
+                    a = 2 * g + a2
+                    nc.tensor.matmul_mx(
+                        out=acc[c, n, g][:, a2, :],
+                        lhsT=wq[c][:, a * P : (a + 1) * P].bitcast(FP8X4),
+                        lhsT_scale=wsc[c][:, a * P : (a + 1) * P],
+                        rhs=xq[c][:, n * HW : (n + 1) * HW].bitcast(FP8X4),
+                        rhs_scale=xsc[c][:, n * HW : (n + 1) * HW],
+                        start=True,
+                        stop=True,
+                    )
+
+        def ox_half(c, a, n, on_vector):
+            if c not in ob:
+                ob[c] = opool.tile([P, NB, 4, HW], F32, name="ob")
+            k = 4 * c + a
+            src = acc[c, n, a // 2][:, a % 2, :]
+            if on_vector:
+                nc.vector.tensor_scalar(out=ob[c][:, n, a, :], in0=src, scalar1=bias_f[:, k : k + 1], scalar2=None, op0=ALU.add)
+            else:
+                nc.scalar.activation(out=ob[c][:, n, a, :], in_=src, func=ACT.Identity, bias=bias_f[:, k : k + 1], scale=1.0)
+
         batch_end = {}
         for b in BATCHES:
             batch_end[b[-1]] = b
@@ -314,18 +346,13 @@ def tile_caps_bn_kernel(tc, x, weight, bias, out):
                 v_sm_b(sm_b_next)
                 sm_b_next = None
             c = i - 1
-            if 0 <= c < NCAP:
-                on_v = [1, 3, 2, 0][: OX_ON_V[c]]
-                last = c == NCAP - 1
-                for a in range(4):
-                    ox(c, a, a in on_v)
-                    if last:
-                        nc.sync.dma_start(out=ova[c, a], in_=ob[c][:, :, a, :])
-                if not last:
-                    nc.sync.dma_start(out=ov[c], in_=ob[c][:].rearrange("p n a w -> p n (a w)"))
-                    if c + UPFRONT < NCAP:
-                        load_x(c + UPFRONT)
-                        load_w(c + UPFRONT)
+            if 0 <= c < NCAP - 2:
+                v_out(c)
+            elif c == NCAP - 1:
+                for n in range(NB):
+                    for a in (0, 2, 1, 3):
+                        ox_half(c, a, n, a >= 2)
+                    nc.sync.dma_start(out=ov[c][:, n, :], in_=ob[c][:, n, :, :].rearrange("p a w -> p (a w)"))
             b = sm_a_next
             sm_a_next = None
             cs = i + ST_LEAD
@@ -334,7 +361,11 @@ def tile_caps_bn_kernel(tc, x, weight, bias, out):
                 v_sm_piece(b, 1)
             if 0 <= i < NCAP:
                 v_xq(i, 1)
-                pe_mm(i)
+                if i < NCAP - 1:
+                    pe_mm(i)
+                else:
+                    pe_mm_half(i, 0)
+                    pe_mm_half(i, 1)
             if 0 <= i + 4 < NCAP:
                 pe_t(i + 4)
             if b is not None:
@@ -347,6 +378,8 @@ def tile_caps_bn_kernel(tc, x, weight, bias, out):
             if b is not None:
                 s_sm(b)
                 sm_b_next = b
+            if i == NCAP - 2:
+                v_out(i)
             if 0 <= i + 1 < NCAP:
                 g_rg(i + 1)
                 s_rg(i + 1)

from contextlib import ExitStack

import concourse.mybir as mybir
from concourse.masks import make_identity

F32 = mybir.dt.float32
BF16 = mybir.dt.bfloat16
U32 = mybir.dt.uint32
U8 = mybir.dt.uint8
FP8X4 = mybir.dt.float8_e4m3fn_x4
ALU = mybir.AluOpType
ACT = mybir.ActivationFunctionType

P = 128
NCAP = 16
D = 512
NB = 2
HW = 256
COLS = NB * HW
EPS = 1e-5
FLOPS = 2 * NCAP * D * D * COLS

BATCHES = [[0], [1]] + [[c, c + 1] for c in range(2, NCAP, 2)]
UPFRONT = 8
ST_LEAD = 4
V_COLS = [0,0,0,0,0,0,0,0,0,0,0,0,0,512,448,448]
G_COLS = [352,352,352,352,352,352,352,352,352,352,352,352,352,0,0,0]
OX_ON_V = [0,0,0,0,0,0,0,0,0,0,0,0,0,1,1,2]


def tile_caps_bn_kernel(tc, x, weight, bias, out):
    nc = tc.nc
    xv = x.rearrange("n (c p t) h w -> c p n (t h w)", c=NCAP, p=P, t=4)
    wv = weight.rearrange("c (m a) i -> c m (a i)", m=P, a=4)
    ov = out.rearrange("n (c m a) h w -> c m n (a h w)", c=NCAP, m=P, a=4)
    bv = bias.rearrange("(c o) -> c o", c=NCAP)

    with ExitStack() as ctx:
        const = ctx.enter_context(tc.tile_pool(name="const", bufs=1))
        xpool = ctx.enter_context(tc.tile_pool(name="xpool", bufs=UPFRONT + 2))
        wpool = ctx.enter_context(tc.tile_pool(name="wpool", bufs=UPFRONT))
        work = ctx.enter_context(tc.tile_pool(name="work", bufs=3))
        small = ctx.enter_context(tc.tile_pool(name="small", bufs=3))
        opool = ctx.enter_context(tc.tile_pool(name="opool", bufs=6))
        pst = ctx.enter_context(tc.psum_pool(name="pst", bufs=4))
        psa = ctx.enter_context(tc.psum_pool(name="psa", bufs=4))
        wqpool = ctx.enter_context(tc.tile_pool(name="wqpool", bufs=4))
        ctx.enter_context(tc.manual_schedule())

        warm = const.tile([P, 2], F32)
        nc.vector.memset(warm[:, 0:1], 1.0)
        nc.scalar.activation(out=warm[:, 1:2], in_=warm[:, 0:1], func=ACT.Sqrt)
        ident = const.tile([P, P], F32)
        make_identity(nc, ident[:])
        bias_rows = const.tile([P, D], BF16)
        nc.vector.memset(bias_rows[:], 0.0)
        bias_am = const.tile([P, 4, P], F32)
        bias_f = const.tile([P, NCAP * 4], F32)
        mean = const.tile([P, NCAP * 4], F32)
        rstd = const.tile([P, NCAP * 4], F32)
        stats = const.tile([P, NCAP * 4, 6], F32)
        sacc = const.tile([P, 4, 2], F32)
        junk = const.tile([P, NB, HW], BF16)

        xs = {}
        ws = {}
        wt = {}
        wg = {}
        wq = {}
        wsc = {}
        xn = {}
        xg = {}
        xq = {}
        xsc = {}
        acc = {}
        ob = {}
        sm = {}

        def load_x(c):
            xs[c] = xpool.tile([P, NB, 4 * HW], BF16, name="xs")
            nc.sync.dma_start(out=xs[c][:], in_=xv[c])

        def load_x_half(c, h):
            if h == 0:
                xs[c] = xpool.tile([P, NB, 4 * HW], BF16, name="xs")
            nc.sync.dma_start(out=xs[c][:, :, 2 * h * HW : 2 * (h + 1) * HW], in_=xv[c][:, :, 2 * h * HW : 2 * (h + 1) * HW])

        def load_w(c):
            ws[c] = wpool.tile([P, 4 * D], BF16, name="ws")
            nc.sync.dma_start(out=ws[c][:], in_=wv[c])

        def s_st(c, t):
            src = xs[c][:, :, t * HW : (t + 1) * HW]
            shift = xs[c][:, 0, t * HW : t * HW + 1]
            nc.scalar.activation(out=junk[:], in_=src, func=ACT.Identity, bias=shift, scale=-1.0, accum_out=sacc[:, t, 0:1])
            nc.scalar.activation(out=junk[:], in_=src, func=ACT.Square, bias=shift, scale=-1.0, accum_out=sacc[:, t, 1:2])

        def v_sm_s(c):
            sm[c, "e"] = small.tile([P, 8], F32, name="sm_e")
            sm[c] = small.tile([P, 8], F32, name="sm_v")
            e = sm[c, "e"][:, 0:4]
            v = sm[c][:, 0:4]
            shifts = xs[c][:, 0, :].rearrange("p (t w) -> p t w", t=4)[:, :, 0]
            nc.vector.scalar_tensor_tensor(out=e, in0=sacc[:, :, 0], scalar=-1.0 / COLS, in1=sacc[:, :, 0], op0=ALU.mult, op1=ALU.mult)
            nc.vector.scalar_tensor_tensor(out=mean[:, 4 * c : 4 * c + 4], in0=sacc[:, :, 0], scalar=-1.0 / COLS, in1=shifts, op0=ALU.mult, op1=ALU.add)
            nc.vector.scalar_tensor_tensor(out=v, in0=sacc[:, :, 1], scalar=COLS * EPS, in1=e, op0=ALU.add, op1=ALU.add)

        def pe_t(c):
            wf = ws[c][:].bitcast(F32).rearrange("p (a q u) -> p a u q", a=4, u=2)
            for h in range(2):
                wt[c, h] = pst.tile([P, 2, 2, P], F32, name="wt")
                for a2 in range(2):
                    for u in range(2):
                        nc.tensor.transpose(wt[c, h][:, a2, u, :], wf[:, 2 * h + a2, u, :], ident[:])

        def s_wx(c):
            wg[c] = work.tile([P, 4 * P * 4], BF16, name="wg", align_bytes=64)
            wgf = wg[c][:].bitcast(F32).rearrange("p (a m u) -> p a m u", a=4, u=2)
            for h in range(2):
                nc.scalar.copy(out=wgf[:, 2 * h : 2 * h + 2, :, :], in_=wt[c, h][:].rearrange("p a u m -> p a m u"))

        def v_wq(c):
            wq[c] = wqpool.tile([P, 4 * P], U32, name="wq", align_bytes=64)
            wsc[c] = wqpool.tile([P, 4 * P], U8, name="wsc", align_bytes=64)
            nc.vector.quantize_mx(out=wq[c][:].bitcast(FP8X4), scales=wsc[c][:], in_=wg[c][:])

        def v_wq_half(c, h):
            if h == 0:
                wq[c] = wqpool.tile([P, 4 * P], U32, name="wq", align_bytes=64)
                wsc[c] = wqpool.tile([P, 4 * P], U8, name="wsc", align_bytes=64)
            nc.vector.quantize_mx(
                out=wq[c][:, 2 * h * P : 2 * (h + 1) * P].bitcast(FP8X4),
                scales=wsc[c][:, 2 * h * P : 2 * (h + 1) * P],
                in_=wg[c][:, 8 * h * P : 8 * (h + 1) * P],
            )

        def v_sm_piece(b, k):
            k0 = 4 * b[0]
            n = 4 * len(b)
            st = stats[:, k0 : k0 + n, :]
            if k == 0:
                sm[b[0], "d"] = small.tile([P, 8], F32, name="sm_d")
                sm[b[0], "e"] = small.tile([P, 8], F32, name="sm_e")
                sm[b[0]] = small.tile([P, 8], F32, name="sm_v")
            d = sm[b[0], "d"][:, 0:n]
            e = sm[b[0], "e"][:, 0:n]
            v = sm[b[0]][:, 0:n]
            if k == 0:
                nc.vector.tensor_tensor(out=d, in0=st[:, :, 1], in1=st[:, :, 4], op=ALU.subtract)
            elif k == 1:
                nc.vector.scalar_tensor_tensor(out=v, in0=st[:, :, 2], scalar=COLS * EPS, in1=st[:, :, 5], op0=ALU.add, op1=ALU.add)
            elif k == 2:
                nc.vector.scalar_tensor_tensor(out=e, in0=d, scalar=COLS / 4.0, in1=d, op0=ALU.mult, op1=ALU.mult)
            elif k == 3:
                nc.vector.scalar_tensor_tensor(out=mean[:, k0 : k0 + n], in0=d, scalar=0.5, in1=st[:, :, 4], op0=ALU.mult, op1=ALU.add)
            else:
                nc.vector.tensor_tensor(out=v, in0=v, in1=e, op=ALU.add)

        def v_st(c, b):
            pieces = [[0, 1], [2, 3], [4], []]
            for t in range(4):
                nc.vector.bn_stats(out=stats[:, 4 * c + t, :], in_=xs[c][:, :, t * HW : (t + 1) * HW])
                if b is not None:
                    for k in pieces[t]:
                        v_sm_piece(b, k)

        def s_sm(b):
            n = 4 * len(b)
            v = sm[b[0]]
            nc.scalar.activation(out=v[:, 0:n], in_=v[:, 0:n], func=ACT.Sqrt, scale=1.0 / COLS)

        def v_sm_b(b):
            k0 = 4 * b[0]
            n = 4 * len(b)
            nc.vector.reciprocal(out=rstd[:, k0 : k0 + n], in_=sm[b[0]][:, 0:n])

        def v_nm(c, b):
            xn[c] = work.tile([P, 4, COLS], BF16, name="xn")
            xg[c] = work.tile([P, COLS, 4], BF16, name="xg", align_bytes=64)
            for t in range(4):
                if t == 1 and b is not None:
                    v_sm_piece(b, 4)
                k = 4 * c + t
                nc.vector.tensor_scalar(
                    out=xn[c][:, t, :].rearrange("p (n w) -> p n w", n=NB),
                    in0=xs[c][:, :, t * HW : (t + 1) * HW],
                    scalar1=mean[:, k : k + 1],
                    scalar2=rstd[:, k : k + 1],
                    op0=ALU.subtract,
                    op1=ALU.mult,
                )

        def rg_views(c, c0, c1):
            dst = xg[c][:, c0:c1, :].rearrange("p (c i) t -> p c t i", i=4)
            src = xn[c][:, :, c0:c1].rearrange("p t (c i) -> p c t i", i=4)
            return dst, src

        def s_rg(c):
            if V_COLS[c] + G_COLS[c] < COLS:
                dst, src = rg_views(c, V_COLS[c] + G_COLS[c], COLS)
                nc.scalar.copy(out=dst, in_=src)

        def g_rg(c):
            if G_COLS[c] > 0:
                c0 = V_COLS[c]
                c1 = c0 + G_COLS[c]
                nc.gpsimd.tensor_scalar(
                    out=xg[c][:, c0:c1, :],
                    in0=xn[c][:, :, c0:c1].rearrange("p t c -> p c t"),
                    scalar1=1.0,
                    scalar2=0.0,
                    op0=ALU.mult,
                    op1=ALU.add,
                )

        def v_rg(c):
            if V_COLS[c] > 0:
                dst, src = rg_views(c, 0, V_COLS[c])
                nc.vector.tensor_copy(out=dst, in_=src)

        def v_xq(c, h):
            if h == 0:
                xq[c] = work.tile([P, COLS], U32, name="xq", align_bytes=64)
                xsc[c] = work.tile([P, COLS], U8, name="xsc", align_bytes=64)
            c0 = h * COLS // 2
            c1 = (h + 1) * COLS // 2
            nc.vector.quantize_mx(
                out=xq[c][:, c0:c1].bitcast(FP8X4),
                scales=xsc[c][:, c0:c1],
                in_=xg[c][:, c0:c1, :].rearrange("p w t -> p (w t)"),
            )

        def pe_mm(c):
            for a in range(4):
                acc[c, a] = psa.tile([P, COLS], F32, name="acc")
                nc.tensor.matmul_mx(
                    out=acc[c, a][:],
                    lhsT=wq[c][:, a * P : (a + 1) * P].bitcast(FP8X4),
                    lhsT_scale=wsc[c][:, a * P : (a + 1) * P],
                    rhs=xq[c][:].bitcast(FP8X4),
                    rhs_scale=xsc[c][:],
                    start=True,
                    stop=True,
                )

        def ox(c, a, on_vector):
            if c not in ob:
                ob[c] = opool.tile([P, NB, 4, HW], F32, name="ob")
            k = 4 * c + a
            src = acc[c, a][:].rearrange("p (n w) -> p n w", n=NB)
            if on_vector:
                nc.vector.tensor_scalar(out=ob[c][:, :, a, :], in0=src, scalar1=bias_f[:, k : k + 1], scalar2=None, op0=ALU.add)
            else:
                nc.scalar.activation(out=ob[c][:, :, a, :], in_=src, func=ACT.Identity, bias=bias_f[:, k : k + 1], scale=1.0)

        def v_out(c):
            for a in range(4):
                ox(c, a, a in [1, 3, 2, 0][: OX_ON_V[c]])
            nc.sync.dma_start(out=ov[c], in_=ob[c][:].rearrange("p n a w -> p n (a w)"))
            if c + UPFRONT < NCAP:
                load_x(c + UPFRONT)
                load_w(c + UPFRONT)

        def pe_mm_half(c, n):
            for g in range(2):
                acc[c, n, g] = psa.tile([P, 2, HW], F32, name="acc")
                for a2 in range(2):
                    a = 2 * g + a2
                    nc.tensor.matmul_mx(
                        out=acc[c, n, g][:, a2, :],
                        lhsT=wq[c][:, a * P : (a + 1) * P].bitcast(FP8X4),
                        lhsT_scale=wsc[c][:, a * P : (a + 1) * P],
                        rhs=xq[c][:, n * HW : (n + 1) * HW].bitcast(FP8X4),
                        rhs_scale=xsc[c][:, n * HW : (n + 1) * HW],
                        start=True,
                        stop=True,
                    )

        def ox_half(c, a, n, on_vector):
            if c not in ob:
                ob[c] = opool.tile([P, NB, 4, HW], F32, name="ob")
            k = 4 * c + a
            src = acc[c, n, a // 2][:, a % 2, :]
            if on_vector:
                nc.vector.tensor_scalar(out=ob[c][:, n, a, :], in0=src, scalar1=bias_f[:, k : k + 1], scalar2=None, op0=ALU.add)
            else:
                nc.scalar.activation(out=ob[c][:, n, a, :], in_=src, func=ACT.Identity, bias=bias_f[:, k : k + 1], scale=1.0)

        batch_end = {}
        for b in BATCHES:
            batch_end[b[-1]] = b

        load_x_half(0, 0)
        nc.sync.dma_start(out=bias_rows[0:NCAP, :], in_=bv)
        load_x_half(1, 0)
        load_x_half(0, 1)
        load_x_half(2, 0)
        load_x_half(1, 1)
        load_x_half(2, 1)
        load_w(0)
        load_x(3)
        load_w(1)
        load_w(2)
        load_x(4)
        load_w(3)
        for c in range(5, UPFRONT):
            load_x(c)
            load_w(c - 1)
        load_w(UPFRONT - 1)

        nc.scalar.copy(out=bias_am[:], in_=bias_rows[:].rearrange("q (m a) -> q a m", a=4))
        bias_t = psa.tile([P, 4, P], F32, name="acc")
        for a in range(4):
            nc.tensor.transpose(bias_t[:, a, :], bias_am[:, a, :], ident[:])
        pe_t(0)
        pe_t(1)
        v_st(0, None)
        s_st(1, 0)
        s_st(1, 1)
        s_st(1, 2)
        v_st(2, [0])
        s_sm([0])
        s_st(1, 3)
        s_wx(0)
        v_sm_b([0])
        v_nm(0, None)
        g_rg(0)
        s_rg(0)
        v_st(3, None)
        pe_t(2)
        s_wx(1)
        pe_t(3)
        v_sm_s(1)
        v_wq(0)
        s_sm([1])
        v_sm_b([1])
        v_wq(1)
        s_wx(2)
        nc.scalar.copy(out=bias_f[:].rearrange("m (c a) -> m c a", a=4), in_=bias_t[:, :, 0:NCAP].rearrange("m a c -> m c a"))
        sm_a_next = [2, 3]
        sm_b_next = None
        for i in range(0, NCAP + 1):
            if 0 <= i < NCAP:
                v_xq(i, 0)
            if sm_b_next is not None:
                v_sm_b(sm_b_next)
                sm_b_next = None
            c = i - 1
            if 0 <= c < NCAP - 2:
                v_out(c)
            elif c == NCAP - 1:
                for n in range(NB):
                    for a in (0, 2, 1, 3):
                        ox_half(c, a, n, a >= 2)
                    nc.sync.dma_start(out=ov[c][:, n, :], in_=ob[c][:, n, :, :].rearrange("p a w -> p (a w)"))
            b = sm_a_next
            sm_a_next = None
            cs = i + ST_LEAD
            if b is not None:
                v_sm_piece(b, 0)
                v_sm_piece(b, 1)
            if 0 <= i < NCAP:
                v_xq(i, 1)
                if i < NCAP - 1:
                    pe_mm(i)
                else:
                    pe_mm_half(i, 0)
                    pe_mm_half(i, 1)
            if 0 <= i + 4 < NCAP:
                pe_t(i + 4)
            if b is not None:
                v_sm_piece(b, 2)
                v_sm_piece(b, 3)
            if i + 1 < NCAP:
                v_nm(i + 1, b)
            if i + 2 < NCAP:
                v_wq(i + 2)
            if b is not None:
                s_sm(b)
                sm_b_next = b
            if i == NCAP - 2:
                v_out(i)
            if 0 <= i + 1 < NCAP:
                g_rg(i + 1)
                s_rg(i + 1)
                v_rg(i + 1)
            if 0 <= i + 1 and cs < NCAP:
                v_st(cs, None)
            if cs < NCAP:
                sm_a_next = batch_end.get(cs)
            if 0 <= i + 3 < NCAP:
                s_wx(i + 3)
